import numpy as np
import ml_dtypes


def mxq(x, axis, fmt="e4m3"):
    dtype, down = {"e4m3": (ml_dtypes.float8_e4m3fn, 7), "e5m2": (ml_dtypes.float8_e5m2, 14)}[fmt]
    v = np.moveaxis(np.asarray(x, np.float32).astype(ml_dtypes.bfloat16).astype(np.float64), axis, -1)
    blocks = v.reshape(v.shape[:-1] + (-1, 32))
    amax = np.abs(blocks).max(-1, keepdims=True)
    byte = np.maximum(np.where(amax > 0, np.frexp(amax)[1] - 1 + 127, 0) - down, 1)
    scale = np.exp2(byte - 127.0)
    codes = (blocks / scale).astype(np.float32).astype(dtype).astype(np.float64)
    return np.moveaxis((codes * scale).reshape(v.shape), -1, axis)


WIDE = False


def mx_kscale(k):
    if not WIDE:
        return np.ones(k)
    levels = np.array([10, -10, 5, -5, 0])
    a = np.random.permutation(np.resize(levels, k // 512 * 4)).reshape(k // 512, 4)
    idx = np.arange(k)
    return np.exp2(a[idx // 512, idx % 128 // 32])


BF16 = ml_dtypes.bfloat16


def bf(x):
    return np.asarray(x, np.float32).astype(BF16)


def f64(x):
    return np.asarray(x).astype(np.float64)


B, T, HID, H, D, QB = 4, 1024, 1024, 4, 128, 512
LN_EPS = 1e-5


def layer_norm(u):
    mu = u.mean(-1, keepdims=True)
    var = ((u - mu) ** 2).mean(-1, keepdims=True)
    return (u - mu) * (1.0 / np.sqrt(var + LN_EPS))


def feature_map(u, gamma, beta):
    return layer_norm(u * gamma + beta)


def setup_inputs():
    s = mx_kscale(HID)
    return {"hidden_states": bf(np.random.standard_normal((B, T, HID)) * s),
            "Wq": bf(np.random.standard_normal((H * D, HID)) / np.sqrt(HID) / s),
            "Wk": bf(np.random.standard_normal((H * D, HID)) / np.sqrt(HID) / s),
            "gamma": bf(1.0 + 0.1 * np.random.standard_normal(D)),
            "beta": bf(0.1 * np.random.standard_normal(D))}


def reference(hidden_states, Wq, Wk, gamma, beta):
    g, b = f64(gamma), f64(beta)
    xq = mxq(f64(hidden_states), 2, "e4m3")
    q = (xq @ mxq(f64(Wq), 1, "e4m3").T).reshape(B, T, H, D)
    k = (xq @ mxq(f64(Wk), 1, "e4m3").T).reshape(B, T, H, D)
    q_feat = feature_map(q, g, b) * (D ** -0.5)
    k_feat = feature_map(k, g, b)
    return q_feat, k_feat

@@ -1,0 +1,276 @@
+from contextlib import ExitStack
+
+import concourse.mybir as mybir
+from concourse.masks import make_identity
+
+F32 = mybir.dt.float32
+BF16 = mybir.dt.bfloat16
+U32 = mybir.dt.uint32
+U8 = mybir.dt.uint8
+FP8X4 = mybir.dt.float8_e4m3fn_x4
+ALU = mybir.AluOpType
+ACT = mybir.ActivationFunctionType
+
+P = 128
+TOKENS = 4 * 1024
+HID = 1024
+HEADS = 4
+D = 128
+LN_EPS = 1e-5
+K_PASS = 4 * P
+PASSES = HID // K_PASS
+WORDS = K_PASS // 2
+GROUP = 512
+N_GROUPS = TOKENS // GROUP
+TILES = GROUP // P
+N_BLOCKS = 2 * N_GROUPS
+N_STEPS = PASSES * N_GROUPS
+ROWS = TILES * HEADS
+
+FLOPS = 2 * TOKENS * HID * 2 * HEADS * D
+
+
+def tile_rebasedlinearattention_pa_t_kernel(tc, hidden_states, Wq, Wk, gamma, beta, out_0, out_1):
+    nc = tc.nc
+    x_dram = hidden_states.rearrange("b t k -> (b t) k").rearrange("(g p t) k -> g p t k", p=P, t=TILES)
+    w_dram = [w.rearrange("(h p) k -> p h k", p=P) for w in (Wq, Wk)]
+    out_dram = [
+        o.rearrange("b t h d -> (b t) (h d)").rearrange("(g p t) f -> g p t f", p=P, t=TILES) for o in (out_0, out_1)
+    ]
+
+    with ExitStack() as stack:
+        const = stack.enter_context(tc.tile_pool(name="const", bufs=1))
+        x_pool = stack.enter_context(tc.tile_pool(name="x", bufs=N_GROUPS))
+        xg_pool = stack.enter_context(tc.tile_pool(name="xg", bufs=3))
+        xc_pool = stack.enter_context(tc.tile_pool(name="xc", bufs=5))
+        ut_pool = stack.enter_context(tc.tile_pool(name="ut", bufs=2))
+        u_pool = stack.enter_context(tc.tile_pool(name="u", bufs=4))
+        f_pool = stack.enter_context(tc.tile_pool(name="f", bufs=4))
+        small = stack.enter_context(tc.tile_pool(name="small", bufs=3))
+        kt_psum = stack.enter_context(tc.psum_pool(name="kt", bufs=2))
+        mx_psum = stack.enter_context(tc.psum_pool(name="mx", bufs=4))
+        bt_psum = stack.enter_context(tc.psum_pool(name="bt", bufs=2))
+        stack.enter_context(tc.manual_schedule())
+
+        gb_rows = const.tile([P, P], BF16)
+        nc.vector.memset(gb_rows[:], 0.0)
+        nc.sync.dma_start(out=gb_rows[0:1, :], in_=gamma.rearrange("(o d) -> o d", o=1))
+        nc.sync.dma_start(out=gb_rows[1:2, :], in_=beta.rearrange("(o d) -> o d", o=1))
+        w_sb = [const.tile([P, HEADS, HID], BF16, name="w_sb%d" % s) for s in range(2)]
+        x_sb = [x_pool.tile([P, TILES, HID], BF16, name="x_sb") for g in range(N_GROUPS)]
+        nc.sync.dma_start(out=w_sb[0][:], in_=w_dram[0])
+        nc.sync.dma_start(out=x_sb[0][:], in_=x_dram[0])
+        nc.sync.dma_start(out=w_sb[1][:], in_=w_dram[1])
+        for g in range(1, N_GROUPS):
+            nc.sync.dma_start(out=x_sb[g][:], in_=x_dram[g])
+
+        ident = const.tile([P, P], F32)
+        make_identity(nc, ident[:])
+        eps_col = const.tile([P, 2], F32)
+        nc.vector.memset(eps_col[:, 0:1], D * LN_EPS)
+        nc.vector.memset(eps_col[:, 1:2], LN_EPS)
+        warm = const.tile([P, 1], F32)
+        nc.scalar.activation(out=warm[:], in_=eps_col[:, 0:1], func=ACT.Sqrt)
+
+        def transpose_pass(rows_a, rows_b, c):
+            bank = kt_psum.tile([P, 2, 2 * P], F32, name="kt")
+            for u in range(2):
+                for r, rows in enumerate((rows_a, rows_b)):
+                    first = c * WORDS + u * P
+                    nc.tensor.transpose(bank[:, u, r * P : (r + 1) * P], rows[:, first : first + P], ident[:])
+            return bank
+
+        def group_words(engine_copy, bank, grouped, first_row):
+            engine_copy(
+                out=grouped.bitcast(F32)[:, first_row : first_row + 2 * P, :], in_=bank[:].rearrange("p u r -> p r u")
+            )
+
+        w_grouped = const.tile([P, PASSES, 2 * HEADS * D, 4], BF16, align_bytes=64)
+        w_codes = const.tile([P, PASSES, 2 * HEADS * D], U32, align_bytes=64)
+        w_scales = const.tile([P, PASSES, 2 * HEADS * D], U8, align_bytes=64)
+
+        def prepare_weights(s):
+            words = w_sb[s][:].bitcast(F32)
+            cols = slice(s * HEADS * D, (s + 1) * HEADS * D)
+            for c in range(PASSES):
+                bank_a = transpose_pass(words[:, 0, :], words[:, 1, :], c)
+                group_words(nc.vector.tensor_copy, bank_a, w_grouped[:, c, :, :], s * HEADS * D)
+                bank_b = transpose_pass(words[:, 2, :], words[:, 3, :], c)
+                group_words(nc.scalar.copy, bank_b, w_grouped[:, c, :, :], s * HEADS * D + 2 * D)
+                nc.vector.quantize_mx(
+                    out=w_codes[:, c, cols].bitcast(FP8X4),
+                    scales=w_scales[:, c, cols],
+                    in_=w_grouped[:, c, cols, :].rearrange("p r t -> p (r t)"),
+                )
+
+        x_banks = {}
+        x_grouped = {}
+        x_codes = {}
+        x_scales = {}
+
+        def tokens_transpose(step):
+            g, c = divmod(step, PASSES)
+            words = x_sb[g][:].bitcast(F32)
+            x_banks[step] = [transpose_pass(words[:, t, :], words[:, t + 1, :], c) for t in range(0, TILES, 2)]
+            x_grouped[step] = xg_pool.tile([P, GROUP, 4], BF16, align_bytes=64, name="x_grouped")
+
+        def tokens_group(step, half):
+            engine_copy = nc.vector.tensor_copy if half == 0 else nc.scalar.copy
+            group_words(engine_copy, x_banks[step][half], x_grouped[step][:], half * 2 * P)
+
+        def tokens_quantise(step):
+            x_codes[step] = xc_pool.tile([P, GROUP], U32, align_bytes=64, name="x_codes")
+            x_scales[step] = xc_pool.tile([P, GROUP], U8, align_bytes=64, name="x_scales")
+            nc.vector.quantize_mx(
+                out=x_codes[step][:].bitcast(FP8X4),
+                scales=x_scales[step][:],
+                in_=x_grouped[step][:].rearrange("p r t -> p (r t)"),
+            )
+
+        u_t = {}
+        u_sb = {}
+        stats = {}
+        sums = {}
+        diff = {}
+        between = {}
+        mean = {}
+        m2 = {}
+        std = {}
+        rstd = {}
+
+        def project(block):
+            g, s = divmod(block, 2)
+            u_t[block] = ut_pool.tile([P, HEADS, GROUP], F32, name="u_t")
+            for h in range(HEADS):
+                cols = slice((s * HEADS + h) * D, (s * HEADS + h + 1) * D)
+                acc = mx_psum.tile([P, GROUP], F32, name="acc")
+                for c in range(PASSES):
+                    nc.tensor.matmul_mx(
+                        out=acc[:],
+                        lhsT=w_codes[:, c, cols].bitcast(FP8X4),
+                        lhsT_scale=w_scales[:, c, cols],
+                        rhs=x_codes[PASSES * g + c][:].bitcast(FP8X4),
+                        rhs_scale=x_scales[PASSES * g + c][:],
+                        start=(c == 0),
+                        stop=(c == PASSES - 1),
+                    )
+                nc.scalar.activation(
+                    out=u_t[block][:, h, :], in_=acc[:], func=ACT.Identity, scale=gb_col[:, 0:1], bias=gb_col[:, 1:2]
+                )
+
+        def tokens_to_partitions(block):
+            u_sb[block] = u_pool.tile([P, TILES, HEADS * D], F32, name="u_sb")
+            for t in range(TILES):
+                bank = bt_psum.tile([P, HEADS * D], F32, name="bank")
+                for h in range(HEADS):
+                    nc.tensor.transpose(bank[:, h * D : (h + 1) * D], u_t[block][:, h, t * P : (t + 1) * P], ident[:])
+                nc.scalar.copy(out=u_sb[block][:, t, :], in_=bank[:])
+
+        def statistics(block):
+            stats[block] = small.tile([P, ROWS, 6], F32, name="stats")
+            for t in range(TILES):
+                for h in range(HEADS):
+                    nc.vector.bn_stats(
+                        out=stats[block][:, t * HEADS + h, :], in_=u_sb[block][:, t, h * D : (h + 1) * D]
+                    )
+
+        def merge_halves(block):
+            halves = stats[block][:].rearrange("p n (e k) -> p n e k", e=2)
+            sums[block] = small.tile([P, ROWS, 3], F32, name="sums")
+            nc.vector.tensor_reduce(
+                out=sums[block][:], in_=halves.rearrange("p n e k -> p n k e"), axis=mybir.AxisListType.X, op=ALU.add
+            )
+            diff[block] = small.tile([P, ROWS], F32, name="diff")
+            nc.vector.tensor_sub(out=diff[block][:], in0=halves[:, :, 0, 1], in1=halves[:, :, 1, 1])
+
+        def mean_and_gap(block):
+            between[block] = small.tile([P, ROWS], F32, name="between")
+            nc.vector.scalar_tensor_tensor(
+                out=between[block][:], in0=diff[block][:], scalar=D / 4.0, in1=diff[block][:], op0=ALU.mult, op1=ALU.mult
+            )
+            mean[block] = small.tile([P, ROWS], F32, name="mean")
+            nc.vector.tensor_scalar_mul(out=mean[block][:], in0=sums[block][:, :, 1], scalar1=0.5)
+
+        def sum_of_squares(block):
+            m2[block] = small.tile([P, ROWS], F32, name="m2")
+            nc.vector.tensor_add(out=m2[block][:], in0=between[block][:], in1=sums[block][:, :, 2])
+
+        def deviation(block):
+            s = block % 2
+            std[block] = small.tile([P, ROWS], F32, name="std")
+            nc.scalar.activation(
+                out=std[block][:],
+                in_=m2[block][:],
+                func=ACT.Sqrt,
+                scale=(1.0 if s == 0 else 1.0 / D),
+                bias=eps_col[:, s : s + 1],
+            )
+
+        def invert(block):
+            rstd[block] = small.tile([P, ROWS], F32, name="rstd")
+            nc.vector.reciprocal(out=rstd[block][:], in_=std[block][:])
+
+        def normalise(block, first_tile):
+            g, s = divmod(block, 2)
+            f_sb = f_pool.tile([P, 2, HEADS * D], F32, name="f_sb")
+            for j in range(2):
+                for h in range(HEADS):
+                    n = (first_tile + j) * HEADS + h
+                    nc.vector.tensor_scalar(
+                        out=f_sb[:, j, h * D : (h + 1) * D],
+                        in0=u_sb[block][:, first_tile + j, h * D : (h + 1) * D],
+                        scalar1=mean[block][:, n : n + 1],
+                        scalar2=rstd[block][:, n : n + 1],
+                        op0=ALU.subtract,
+                        op1=ALU.mult,
+                    )
+            nc.sync.dma_start(out=out_dram[s][g][:, first_tile : first_tile + 2, :], in_=f_sb[:])
+
+        prepare_weights(0)
+        for step in range(PASSES):
+            tokens_transpose(step)
+            tokens_group(step, 0)
+            tokens_group(step, 1)
+            tokens_quantise(step)
+        gb_f32 = const.tile([P, P], F32)
+        nc.vector.tensor_copy(out=gb_f32[:], in_=gb_rows[:])
+        gb_bank = kt_psum.tile([P, 2, 2 * P], F32, name="kt")
+        nc.tensor.transpose(gb_bank[:, 0, 0:P], gb_f32[:], ident[:])
+        gb_col = const.tile([P, 2], F32)
+        nc.vector.tensor_copy(out=gb_col[:], in_=gb_bank[:, 0, 0:2])
+        prepare_weights(1)
+        tokens_transpose(PASSES)
+        tokens_group(PASSES, 0)
+        tokens_group(PASSES, 1)
+
+        def is_block(b):
+            return 0 <= b < N_BLOCKS
+
+        for i in range(N_BLOCKS + 2):
+            ahead = i + PASSES + 1
+            if is_block(i - 2):
+                deviation(i - 2)
+            if is_block(i):
+                project(i)
+            if ahead < N_STEPS:
+                tokens_transpose(ahead)
+                tokens_group(ahead, 1)
+            if is_block(i):
+                tokens_to_partitions(i)
+            if is_block(i - 2):
+                invert(i - 2)
+            if ahead - 1 < N_STEPS:
+                tokens_quantise(ahead - 1)
+            if is_block(i - 1):
+                statistics(i - 1)
+            if ahead < N_STEPS:
+                tokens_group(ahead, 0)
+            if is_block(i - 1):
+                merge_halves(i - 1)
+            if is_block(i - 2):
+                normalise(i - 2, 0)
+            if is_block(i - 1):
+                mean_and_gap(i - 1)
+                sum_of_squares(i - 1)
+            if is_block(i - 2):
+                normalise(i - 2, 2)

@@ -26,6 +26,10 @@ TILES = GROUP // P
 N_BLOCKS = 2 * N_GROUPS
 N_STEPS = PASSES * N_GROUPS
 ROWS = TILES * HEADS
+RUN = 2
+ROUNDS = HEADS // RUN
+N_ROUNDS = N_BLOCKS * ROUNDS
+N_BANKS = 2 * N_STEPS
 
 FLOPS = 2 * TOKENS * HID * 2 * HEADS * D
 
@@ -48,8 +52,8 @@ def tile_rebasedlinearattention_pa_t_kernel(tc, hidden_states, Wq, Wk, gamma, be
         f_pool = stack.enter_context(tc.tile_pool(name="f", bufs=4))
         small = stack.enter_context(tc.tile_pool(name="small", bufs=3))
         kt_psum = stack.enter_context(tc.psum_pool(name="kt", bufs=2))
-        mx_psum = stack.enter_context(tc.psum_pool(name="mx", bufs=4))
-        bt_psum = stack.enter_context(tc.psum_pool(name="bt", bufs=2))
+        mx_psum = stack.enter_context(tc.psum_pool(name="mx", bufs=3))
+        bt_psum = stack.enter_context(tc.psum_pool(name="bt", bufs=3))
         stack.enter_context(tc.manual_schedule())
 
         gb_rows = const.tile([P, P], BF16)
@@ -108,15 +112,18 @@ def tile_rebasedlinearattention_pa_t_kernel(tc, hidden_states, Wq, Wk, gamma, be
         x_codes = {}
         x_scales = {}
 
-        def tokens_transpose(step):
+        def tokens_transpose(bank):
+            step, half = divmod(bank, 2)
             g, c = divmod(step, PASSES)
             words = x_sb[g][:].bitcast(F32)
-            x_banks[step] = [transpose_pass(words[:, t, :], words[:, t + 1, :], c) for t in range(0, TILES, 2)]
-            x_grouped[step] = xg_pool.tile([P, GROUP, 4], BF16, align_bytes=64, name="x_grouped")
+            x_banks[bank] = transpose_pass(words[:, 2 * half, :], words[:, 2 * half + 1, :], c)
+            if half == 0:
+                x_grouped[step] = xg_pool.tile([P, GROUP, 4], BF16, align_bytes=64, name="x_grouped")
 
-        def tokens_group(step, half):
+        def tokens_group(bank):
+            step, half = divmod(bank, 2)
             engine_copy = nc.vector.tensor_copy if half == 0 else nc.scalar.copy
-            group_words(engine_copy, x_banks[step][half], x_grouped[step][:], half * 2 * P)
+            group_words(engine_copy, x_banks[bank], x_grouped[step][:], half * 2 * P)
 
         def tokens_quantise(step):
             x_codes[step] = xc_pool.tile([P, GROUP], U32, align_bytes=64, name="x_codes")
@@ -138,10 +145,11 @@ def tile_rebasedlinearattention_pa_t_kernel(tc, hidden_states, Wq, Wk, gamma, be
         std = {}
         rstd = {}
 
-        def project(block):
+        def project(block, first_head):
             g, s = divmod(block, 2)
-            u_t[block] = ut_pool.tile([P, HEADS, GROUP], F32, name="u_t")
-            for h in range(HEADS):
+            if first_head == 0:
+                u_t[block] = ut_pool.tile([P, HEADS, GROUP], F32, name="u_t")
+            for h in range(first_head, first_head + RUN):
                 cols = slice((s * HEADS + h) * D, (s * HEADS + h + 1) * D)
                 acc = mx_psum.tile([P, GROUP], F32, name="acc")
                 for c in range(PASSES):
@@ -158,21 +166,20 @@ def tile_rebasedlinearattention_pa_t_kernel(tc, hidden_states, Wq, Wk, gamma, be
                     out=u_t[block][:, h, :], in_=acc[:], func=ACT.Identity, scale=gb_col[:, 0:1], bias=gb_col[:, 1:2]
                 )
 
-        def tokens_to_partitions(block):
-            u_sb[block] = u_pool.tile([P, TILES, HEADS * D], F32, name="u_sb")
-            for t in range(TILES):
+        def tokens_to_partitions(block, first_tile):
+            if first_tile == 0:
+                u_sb[block] = u_pool.tile([P, TILES, HEADS * D], F32, name="u_sb")
+            for t in range(first_tile, first_tile + RUN):
                 bank = bt_psum.tile([P, HEADS * D], F32, name="bank")
                 for h in range(HEADS):
                     nc.tensor.transpose(bank[:, h * D : (h + 1) * D], u_t[block][:, h, t * P : (t + 1) * P], ident[:])
                 nc.scalar.copy(out=u_sb[block][:, t, :], in_=bank[:])
 
-        def statistics(block):
-            stats[block] = small.tile([P, ROWS, 6], F32, name="stats")
-            for t in range(TILES):
-                for h in range(HEADS):
-                    nc.vector.bn_stats(
-                        out=stats[block][:, t * HEADS + h, :], in_=u_sb[block][:, t, h * D : (h + 1) * D]
-                    )
+        def statistics(block, t):
+            if t == 0:
+                stats[block] = small.tile([P, ROWS, 6], F32, name="stats")
+            for h in range(HEADS):
+                nc.vector.bn_stats(out=stats[block][:, t * HEADS + h, :], in_=u_sb[block][:, t, h * D : (h + 1) * D])
 
         def merge_halves(block):
             halves = stats[block][:].rearrange("p n (e k) -> p n e k", e=2)
@@ -212,8 +219,8 @@ def tile_rebasedlinearattention_pa_t_kernel(tc, hidden_states, Wq, Wk, gamma, be
 
         def normalise(block, first_tile):
             g, s = divmod(block, 2)
-            f_sb = f_pool.tile([P, 2, HEADS * D], F32, name="f_sb")
-            for j in range(2):
+            f_sb = f_pool.tile([P, RUN, HEADS * D], F32, name="f_sb")
+            for j in range(RUN):
                 for h in range(HEADS):
                     n = (first_tile + j) * HEADS + h
                     nc.vector.tensor_scalar(
@@ -224,14 +231,14 @@ def tile_rebasedlinearattention_pa_t_kernel(tc, hidden_states, Wq, Wk, gamma, be
                         op0=ALU.subtract,
                         op1=ALU.mult,
                     )
-            nc.sync.dma_start(out=out_dram[s][g][:, first_tile : first_tile + 2, :], in_=f_sb[:])
+            nc.sync.dma_start(out=out_dram[s][g][:, first_tile : first_tile + RUN, :], in_=f_sb[:])
 
         prepare_weights(0)
-        for step in range(PASSES):
-            tokens_transpose(step)
-            tokens_group(step, 0)
-            tokens_group(step, 1)
-            tokens_quantise(step)
+        for bank in range(2 * PASSES):
+            tokens_transpose(bank)
+            tokens_group(bank)
+            if bank % 2 == 1:
+                tokens_quantise(bank // 2)
         gb_f32 = const.tile([P, P], F32)
         nc.vector.tensor_copy(out=gb_f32[:], in_=gb_rows[:])
         gb_bank = kt_psum.tile([P, 2, 2 * P], F32, name="kt")
@@ -239,38 +246,49 @@ def tile_rebasedlinearattention_pa_t_kernel(tc, hidden_states, Wq, Wk, gamma, be
         gb_col = const.tile([P, 2], F32)
         nc.vector.tensor_copy(out=gb_col[:], in_=gb_bank[:, 0, 0:2])
         prepare_weights(1)
-        tokens_transpose(PASSES)
-        tokens_group(PASSES, 0)
-        tokens_group(PASSES, 1)
+        BANKS_AHEAD = 2 * PASSES + 2
+        for bank in range(2 * PASSES, BANKS_AHEAD):
+            tokens_transpose(bank)
+            tokens_group(bank)
 
-        def is_block(b):
-            return 0 <= b < N_BLOCKS
+        def part_of_block(r):
+            if 0 <= r < N_ROUNDS:
+                return r // ROUNDS, (r % ROUNDS) * RUN
+            return None
 
-        for i in range(N_BLOCKS + 2):
-            ahead = i + PASSES + 1
-            if is_block(i - 2):
-                deviation(i - 2)
-            if is_block(i):
-                project(i)
-            if ahead < N_STEPS:
-                tokens_transpose(ahead)
-                tokens_group(ahead, 1)
-            if is_block(i):
-                tokens_to_partitions(i)
-            if is_block(i - 2):
-                invert(i - 2)
-            if ahead - 1 < N_STEPS:
-                tokens_quantise(ahead - 1)
-            if is_block(i - 1):
-                statistics(i - 1)
-            if ahead < N_STEPS:
-                tokens_group(ahead, 0)
-            if is_block(i - 1):
-                merge_halves(i - 1)
-            if is_block(i - 2):
-                normalise(i - 2, 0)
-            if is_block(i - 1):
-                mean_and_gap(i - 1)
-                sum_of_squares(i - 1)
-            if is_block(i - 2):
-                normalise(i - 2, 2)
+        def whole_block(r):
+            if 0 <= r < N_ROUNDS and r % ROUNDS == 0:
+                return r // ROUNDS
+            return None
+
+        for j in range(N_ROUNDS + 7):
+            bank = j + BANKS_AHEAD
+            if whole_block(j - 6) is not None:
+                deviation(whole_block(j - 6))
+            if part_of_block(j) is not None:
+                project(*part_of_block(j))
+            if part_of_block(j - 2) is not None:
+                tokens_to_partitions(*part_of_block(j - 2))
+            if bank < N_BANKS:
+                tokens_transpose(bank)
+                if bank % 2 == 1:
+                    tokens_group(bank)
+            if bank % 2 == 0 and bank // 2 - 1 < N_STEPS:
+                tokens_quantise(bank // 2 - 1)
+            if part_of_block(j - 3) is not None:
+                block, first_tile = part_of_block(j - 3)
+                statistics(block, first_tile)
+            if whole_block(j - 5) is not None:
+                mean_and_gap(whole_block(j - 5))
+                sum_of_squares(whole_block(j - 5))
+            if part_of_block(j - 3) is not None:
+                block, first_tile = part_of_block(j - 3)
+                statistics(block, first_tile + 1)
+            if whole_block(j - 4) is not None:
+                merge_halves(whole_block(j - 4))
+            if bank < N_BANKS and bank % 2 == 0:
+                tokens_group(bank)
+            if part_of_block(j - 7) is not None:
+                normalise(*part_of_block(j - 7))
+            if whole_block(j - 6) is not None:
+                invert(whole_block(j - 6))

@@ -24,12 +24,12 @@ GROUP = 512
 N_GROUPS = TOKENS // GROUP
 TILES = GROUP // P
 N_BLOCKS = 2 * N_GROUPS
-N_STEPS = PASSES * N_GROUPS
 ROWS = TILES * HEADS
 RUN = 2
 ROUNDS = HEADS // RUN
 N_ROUNDS = N_BLOCKS * ROUNDS
-N_BANKS = 2 * N_STEPS
+JOBS_FIRST = 8
+JOBS_PER_ROUND = 3
 
 FLOPS = 2 * TOKENS * HID * 2 * HEADS * D
 
@@ -44,29 +44,50 @@ def tile_rebasedlinearattention_pa_t_kernel(tc, hidden_states, Wq, Wk, gamma, be
 
     with ExitStack() as stack:
         const = stack.enter_context(tc.tile_pool(name="const", bufs=1))
-        x_pool = stack.enter_context(tc.tile_pool(name="x", bufs=N_GROUPS))
-        xg_pool = stack.enter_context(tc.tile_pool(name="xg", bufs=3))
-        xc_pool = stack.enter_context(tc.tile_pool(name="xc", bufs=5))
+        raw_pool = stack.enter_context(tc.tile_pool(name="raw", bufs=10))
+        grouped_pool = stack.enter_context(tc.tile_pool(name="grouped", bufs=6))
         ut_pool = stack.enter_context(tc.tile_pool(name="ut", bufs=2))
         u_pool = stack.enter_context(tc.tile_pool(name="u", bufs=4))
         f_pool = stack.enter_context(tc.tile_pool(name="f", bufs=4))
         small = stack.enter_context(tc.tile_pool(name="small", bufs=3))
-        kt_psum = stack.enter_context(tc.psum_pool(name="kt", bufs=2))
-        mx_psum = stack.enter_context(tc.psum_pool(name="mx", bufs=3))
+        kt_psum = stack.enter_context(tc.psum_pool(name="kt", bufs=3))
+        mx_psum = stack.enter_context(tc.psum_pool(name="mx", bufs=2))
         bt_psum = stack.enter_context(tc.psum_pool(name="bt", bufs=3))
         stack.enter_context(tc.manual_schedule())
+
+        w_codes = const.tile([P, PASSES, 2 * HEADS * D], U32, align_bytes=64)
+        w_scales = const.tile([P, PASSES, 2 * HEADS * D], U8, align_bytes=64)
+        x_codes = const.tile([P, N_GROUPS, PASSES, GROUP], U32, align_bytes=64)
+        x_scales = const.tile([P, N_GROUPS, PASSES, GROUP], U8, align_bytes=64)
 
         gb_rows = const.tile([P, P], BF16)
         nc.vector.memset(gb_rows[:], 0.0)
         nc.sync.dma_start(out=gb_rows[0:1, :], in_=gamma.rearrange("(o d) -> o d", o=1))
         nc.sync.dma_start(out=gb_rows[1:2, :], in_=beta.rearrange("(o d) -> o d", o=1))
-        w_sb = [const.tile([P, HEADS, HID], BF16, name="w_sb%d" % s) for s in range(2)]
-        x_sb = [x_pool.tile([P, TILES, HID], BF16, name="x_sb") for g in range(N_GROUPS)]
-        nc.sync.dma_start(out=w_sb[0][:], in_=w_dram[0])
-        nc.sync.dma_start(out=x_sb[0][:], in_=x_dram[0])
-        nc.sync.dma_start(out=w_sb[1][:], in_=w_dram[1])
+
+        jobs = []
+
+        def load_rows(rows_dram, codes, scales):
+            raw = raw_pool.tile([P, 2, HID], BF16, name="raw")
+            nc.sync.dma_start(out=raw[:], in_=rows_dram)
+            for c in range(PASSES):
+                jobs.append((raw[:].bitcast(F32), c, codes[:, c, :], scales[:, c, :]))
+
+        def load_tokens(g):
+            for t in range(0, TILES, 2):
+                cols = slice(t * P, (t + 2) * P)
+                load_rows(x_dram[g][:, t : t + 2, :], x_codes[:, g, :, cols], x_scales[:, g, :, cols])
+
+        def load_weights(s):
+            for h in range(0, HEADS, 2):
+                cols = slice((s * HEADS + h) * D, (s * HEADS + h + 2) * D)
+                load_rows(w_dram[s][:, h : h + 2, :], w_codes[:, :, cols], w_scales[:, :, cols])
+
+        load_tokens(0)
+        load_weights(0)
+        load_weights(1)
         for g in range(1, N_GROUPS):
-            nc.sync.dma_start(out=x_sb[g][:], in_=x_dram[g])
+            load_tokens(g)
 
         ident = const.tile([P, P], F32)
         make_identity(nc, ident[:])
@@ -76,70 +97,31 @@ def tile_rebasedlinearattention_pa_t_kernel(tc, hidden_states, Wq, Wk, gamma, be
         warm = const.tile([P, 1], F32)
         nc.scalar.activation(out=warm[:], in_=eps_col[:, 0:1], func=ACT.Sqrt)
 
-        def transpose_pass(rows_a, rows_b, c):
-            bank = kt_psum.tile([P, 2, 2 * P], F32, name="kt")
+        job_bank = {}
+        job_grouped = {}
+
+        def job_transpose(n):
+            words, c, codes, scales = jobs[n]
+            job_bank[n] = kt_psum.tile([P, 2, 2 * P], F32, name="kt")
             for u in range(2):
-                for r, rows in enumerate((rows_a, rows_b)):
+                for r in range(2):
                     first = c * WORDS + u * P
-                    nc.tensor.transpose(bank[:, u, r * P : (r + 1) * P], rows[:, first : first + P], ident[:])
-            return bank
+                    nc.tensor.transpose(job_bank[n][:, u, r * P : (r + 1) * P], words[:, r, first : first + P], ident[:])
 
-        def group_words(engine_copy, bank, grouped, first_row):
-            engine_copy(
-                out=grouped.bitcast(F32)[:, first_row : first_row + 2 * P, :], in_=bank[:].rearrange("p u r -> p r u")
-            )
+        def job_group(n):
+            job_grouped[n] = grouped_pool.tile([P, 2 * P, 4], BF16, align_bytes=64, name="grouped")
+            engine_copy = nc.vector.tensor_copy if n % 2 == 0 else nc.scalar.copy
+            engine_copy(out=job_grouped[n][:].bitcast(F32), in_=job_bank[n][:].rearrange("p u r -> p r u"))
 
-        w_grouped = const.tile([P, PASSES, 2 * HEADS * D, 4], BF16, align_bytes=64)
-        w_codes = const.tile([P, PASSES, 2 * HEADS * D], U32, align_bytes=64)
-        w_scales = const.tile([P, PASSES, 2 * HEADS * D], U8, align_bytes=64)
-
-        def prepare_weights(s):
-            words = w_sb[s][:].bitcast(F32)
-            cols = slice(s * HEADS * D, (s + 1) * HEADS * D)
-            for c in range(PASSES):
-                bank_a = transpose_pass(words[:, 0, :], words[:, 1, :], c)
-                group_words(nc.vector.tensor_copy, bank_a, w_grouped[:, c, :, :], s * HEADS * D)
-                bank_b = transpose_pass(words[:, 2, :], words[:, 3, :], c)
-                group_words(nc.scalar.copy, bank_b, w_grouped[:, c, :, :], s * HEADS * D + 2 * D)
-                nc.vector.quantize_mx(
-                    out=w_codes[:, c, cols].bitcast(FP8X4),
-                    scales=w_scales[:, c, cols],
-                    in_=w_grouped[:, c, cols, :].rearrange("p r t -> p (r t)"),
-                )
-
-        x_banks = {}
-        x_grouped = {}
-        x_codes = {}
-        x_scales = {}
-
-        def tokens_transpose(bank):
-            step, half = divmod(bank, 2)
-            g, c = divmod(step, PASSES)
-            words = x_sb[g][:].bitcast(F32)
-            x_banks[bank] = transpose_pass(words[:, 2 * half, :], words[:, 2 * half + 1, :], c)
-            if half == 0:
-                x_grouped[step] = xg_pool.tile([P, GROUP, 4], BF16, align_bytes=64, name="x_grouped")
-
-        def tokens_group(bank):
-            step, half = divmod(bank, 2)
-            engine_copy = nc.vector.tensor_copy if half == 0 else nc.scalar.copy
-            group_words(engine_copy, x_banks[bank], x_grouped[step][:], half * 2 * P)
-
-        def tokens_quantise(step):
-            x_codes[step] = xc_pool.tile([P, GROUP], U32, align_bytes=64, name="x_codes")
-            x_scales[step] = xc_pool.tile([P, GROUP], U8, align_bytes=64, name="x_scales")
+        def job_quantise(n):
+            words, c, codes, scales = jobs[n]
             nc.vector.quantize_mx(
-                out=x_codes[step][:].bitcast(FP8X4),
-                scales=x_scales[step][:],
-                in_=x_grouped[step][:].rearrange("p r t -> p (r t)"),
+                out=codes.bitcast(FP8X4), scales=scales, in_=job_grouped[n][:].rearrange("p r t -> p (r t)")
             )
 
         u_t = {}
         u_sb = {}
         stats = {}
-        sums = {}
-        diff = {}
-        between = {}
         mean = {}
         m2 = {}
         std = {}
@@ -157,8 +139,8 @@ def tile_rebasedlinearattention_pa_t_kernel(tc, hidden_states, Wq, Wk, gamma, be
                         out=acc[:],
                         lhsT=w_codes[:, c, cols].bitcast(FP8X4),
                         lhsT_scale=w_scales[:, c, cols],
-                        rhs=x_codes[PASSES * g + c][:].bitcast(FP8X4),
-                        rhs_scale=x_scales[PASSES * g + c][:],
+                        rhs=x_codes[:, g, c, :].bitcast(FP8X4),
+                        rhs_scale=x_scales[:, g, c, :],
                         start=(c == 0),
                         stop=(c == PASSES - 1),
                     )
@@ -175,32 +157,35 @@ def tile_rebasedlinearattention_pa_t_kernel(tc, hidden_states, Wq, Wk, gamma, be
                     nc.tensor.transpose(bank[:, h * D : (h + 1) * D], u_t[block][:, h, t * P : (t + 1) * P], ident[:])
                 nc.scalar.copy(out=u_sb[block][:, t, :], in_=bank[:])
 
-        def statistics(block, t):
-            if t == 0:
+        def statistics(block, first_tile):
+            if first_tile == 0:
                 stats[block] = small.tile([P, ROWS, 6], F32, name="stats")
-            for h in range(HEADS):
-                nc.vector.bn_stats(out=stats[block][:, t * HEADS + h, :], in_=u_sb[block][:, t, h * D : (h + 1) * D])
+            for t in range(first_tile, first_tile + RUN):
+                for h in range(HEADS):
+                    nc.vector.bn_stats(
+                        out=stats[block][:, t * HEADS + h, :], in_=u_sb[block][:, t, h * D : (h + 1) * D]
+                    )
 
         def merge_halves(block):
             halves = stats[block][:].rearrange("p n (e k) -> p n e k", e=2)
-            sums[block] = small.tile([P, ROWS, 3], F32, name="sums")
-            nc.vector.tensor_reduce(
-                out=sums[block][:], in_=halves.rearrange("p n e k -> p n k e"), axis=mybir.AxisListType.X, op=ALU.add
+            mean_sum = small.tile([P, ROWS], F32, name="mean_sum")
+            nc.gpsimd.tensor_add(out=mean_sum[:], in0=halves[:, :, 0, 1], in1=halves[:, :, 1, 1])
+            gap = small.tile([P, ROWS], F32, name="gap")
+            nc.gpsimd.tensor_sub(out=gap[:], in0=halves[:, :, 0, 1], in1=halves[:, :, 1, 1])
+            within = small.tile([P, ROWS], F32, name="within")
+            nc.gpsimd.tensor_add(out=within[:], in0=halves[:, :, 0, 2], in1=halves[:, :, 1, 2])
+            gap_scaled = small.tile([P, ROWS], F32, name="gap_scaled")
+            nc.gpsimd.tensor_scalar(
+                out=gap_scaled[:], in0=gap[:], scalar1=D / 4.0, scalar2=0.0, op0=ALU.mult, op1=ALU.add
             )
-            diff[block] = small.tile([P, ROWS], F32, name="diff")
-            nc.vector.tensor_sub(out=diff[block][:], in0=halves[:, :, 0, 1], in1=halves[:, :, 1, 1])
-
-        def mean_and_gap(block):
-            between[block] = small.tile([P, ROWS], F32, name="between")
-            nc.vector.scalar_tensor_tensor(
-                out=between[block][:], in0=diff[block][:], scalar=D / 4.0, in1=diff[block][:], op0=ALU.mult, op1=ALU.mult
-            )
-            mean[block] = small.tile([P, ROWS], F32, name="mean")
-            nc.vector.tensor_scalar_mul(out=mean[block][:], in0=sums[block][:, :, 1], scalar1=0.5)
-
-        def sum_of_squares(block):
+            between = small.tile([P, ROWS], F32, name="between")
+            nc.gpsimd.tensor_mul(out=between[:], in0=gap_scaled[:], in1=gap[:])
             m2[block] = small.tile([P, ROWS], F32, name="m2")
-            nc.vector.tensor_add(out=m2[block][:], in0=between[block][:], in1=sums[block][:, :, 2])
+            nc.gpsimd.tensor_add(out=m2[block][:], in0=between[:], in1=within[:])
+            mean[block] = small.tile([P, ROWS], F32, name="mean")
+            nc.gpsimd.tensor_scalar(
+                out=mean[block][:], in0=mean_sum[:], scalar1=0.5, scalar2=0.0, op0=ALU.mult, op1=ALU.add
+            )
 
         def deviation(block):
             s = block % 2
@@ -233,23 +218,17 @@ def tile_rebasedlinearattention_pa_t_kernel(tc, hidden_states, Wq, Wk, gamma, be
                     )
             nc.sync.dma_start(out=out_dram[s][g][:, first_tile : first_tile + RUN, :], in_=f_sb[:])
 
-        prepare_weights(0)
-        for bank in range(2 * PASSES):
-            tokens_transpose(bank)
-            tokens_group(bank)
-            if bank % 2 == 1:
-                tokens_quantise(bank // 2)
+        for n in range(JOBS_FIRST):
+            job_transpose(n)
+            job_group(n)
+            if n > 0:
+                job_quantise(n - 1)
         gb_f32 = const.tile([P, P], F32)
         nc.vector.tensor_copy(out=gb_f32[:], in_=gb_rows[:])
         gb_bank = kt_psum.tile([P, 2, 2 * P], F32, name="kt")
         nc.tensor.transpose(gb_bank[:, 0, 0:P], gb_f32[:], ident[:])
         gb_col = const.tile([P, 2], F32)
         nc.vector.tensor_copy(out=gb_col[:], in_=gb_bank[:, 0, 0:2])
-        prepare_weights(1)
-        BANKS_AHEAD = 2 * PASSES + 2
-        for bank in range(2 * PASSES, BANKS_AHEAD):
-            tokens_transpose(bank)
-            tokens_group(bank)
 
         def part_of_block(r):
             if 0 <= r < N_ROUNDS:
@@ -261,33 +240,32 @@ def tile_rebasedlinearattention_pa_t_kernel(tc, hidden_states, Wq, Wk, gamma, be
                 return r // ROUNDS
             return None
 
+        done = JOBS_FIRST
+        quantised = JOBS_FIRST - 1
         for j in range(N_ROUNDS + 7):
-            bank = j + BANKS_AHEAD
+            fresh = range(done, min(done + JOBS_PER_ROUND, len(jobs)))
             if whole_block(j - 6) is not None:
                 deviation(whole_block(j - 6))
             if part_of_block(j) is not None:
                 project(*part_of_block(j))
             if part_of_block(j - 2) is not None:
                 tokens_to_partitions(*part_of_block(j - 2))
-            if bank < N_BANKS:
-                tokens_transpose(bank)
-                if bank % 2 == 1:
-                    tokens_group(bank)
-            if bank % 2 == 0 and bank // 2 - 1 < N_STEPS:
-                tokens_quantise(bank // 2 - 1)
+            for n in fresh:
+                job_transpose(n)
+            for n in fresh:
+                if n % 2 == 1:
+                    job_group(n)
+            for n in range(quantised, done):
+                job_quantise(n)
+            quantised = done
+            done = done + len(fresh)
             if part_of_block(j - 3) is not None:
-                block, first_tile = part_of_block(j - 3)
-                statistics(block, first_tile)
-            if whole_block(j - 5) is not None:
-                mean_and_gap(whole_block(j - 5))
-                sum_of_squares(whole_block(j - 5))
-            if part_of_block(j - 3) is not None:
-                block, first_tile = part_of_block(j - 3)
-                statistics(block, first_tile + 1)
+                statistics(*part_of_block(j - 3))
             if whole_block(j - 4) is not None:
                 merge_halves(whole_block(j - 4))
-            if bank < N_BANKS and bank % 2 == 0:
-                tokens_group(bank)
+            for n in fresh:
+                if n % 2 == 0:
+                    job_group(n)
             if part_of_block(j - 7) is not None:
                 normalise(*part_of_block(j - 7))
             if whole_block(j - 6) is not None:

@@ -48,7 +48,7 @@ def tile_rebasedlinearattention_pa_t_kernel(tc, hidden_states, Wq, Wk, gamma, be
         grouped_pool = stack.enter_context(tc.tile_pool(name="grouped", bufs=6))
         ut_pool = stack.enter_context(tc.tile_pool(name="ut", bufs=2))
         u_pool = stack.enter_context(tc.tile_pool(name="u", bufs=4))
-        f_pool = stack.enter_context(tc.tile_pool(name="f", bufs=4))
+        f_pool = stack.enter_context(tc.tile_pool(name="f", bufs=8))
         small = stack.enter_context(tc.tile_pool(name="small", bufs=3))
         kt_psum = stack.enter_context(tc.psum_pool(name="kt", bufs=3))
         mx_psum = stack.enter_context(tc.psum_pool(name="mx", bufs=2))
@@ -59,11 +59,6 @@ def tile_rebasedlinearattention_pa_t_kernel(tc, hidden_states, Wq, Wk, gamma, be
         w_scales = const.tile([P, PASSES, 2 * HEADS * D], U8, align_bytes=64)
         x_codes = const.tile([P, N_GROUPS, PASSES, GROUP], U32, align_bytes=64)
         x_scales = const.tile([P, N_GROUPS, PASSES, GROUP], U8, align_bytes=64)
-
-        gb_rows = const.tile([P, P], BF16)
-        nc.vector.memset(gb_rows[:], 0.0)
-        nc.sync.dma_start(out=gb_rows[0:1, :], in_=gamma.rearrange("(o d) -> o d", o=1))
-        nc.sync.dma_start(out=gb_rows[1:2, :], in_=beta.rearrange("(o d) -> o d", o=1))
 
         jobs = []
 
@@ -85,6 +80,10 @@ def tile_rebasedlinearattention_pa_t_kernel(tc, hidden_states, Wq, Wk, gamma, be
 
         load_tokens(0)
         load_weights(0)
+        gb_rows = const.tile([P, P], BF16)
+        nc.vector.memset(gb_rows[:], 0.0)
+        nc.sync.dma_start(out=gb_rows[0:1, :], in_=gamma.rearrange("(o d) -> o d", o=1))
+        nc.sync.dma_start(out=gb_rows[1:2, :], in_=beta.rearrange("(o d) -> o d", o=1))
         load_weights(1)
         for g in range(1, N_GROUPS):
             load_tokens(g)
@@ -168,8 +167,6 @@ def tile_rebasedlinearattention_pa_t_kernel(tc, hidden_states, Wq, Wk, gamma, be
 
         def merge_halves(block):
             halves = stats[block][:].rearrange("p n (e k) -> p n e k", e=2)
-            mean_sum = small.tile([P, ROWS], F32, name="mean_sum")
-            nc.gpsimd.tensor_add(out=mean_sum[:], in0=halves[:, :, 0, 1], in1=halves[:, :, 1, 1])
             gap = small.tile([P, ROWS], F32, name="gap")
             nc.gpsimd.tensor_sub(out=gap[:], in0=halves[:, :, 0, 1], in1=halves[:, :, 1, 1])
             within = small.tile([P, ROWS], F32, name="within")
@@ -182,6 +179,8 @@ def tile_rebasedlinearattention_pa_t_kernel(tc, hidden_states, Wq, Wk, gamma, be
             nc.gpsimd.tensor_mul(out=between[:], in0=gap_scaled[:], in1=gap[:])
             m2[block] = small.tile([P, ROWS], F32, name="m2")
             nc.gpsimd.tensor_add(out=m2[block][:], in0=between[:], in1=within[:])
+            mean_sum = small.tile([P, ROWS], F32, name="mean_sum")
+            nc.gpsimd.tensor_add(out=mean_sum[:], in0=halves[:, :, 0, 1], in1=halves[:, :, 1, 1])
             mean[block] = small.tile([P, ROWS], F32, name="mean")
             nc.gpsimd.tensor_scalar(
                 out=mean[block][:], in0=mean_sum[:], scalar1=0.5, scalar2=0.0, op0=ALU.mult, op1=ALU.add
@@ -204,19 +203,19 @@ def tile_rebasedlinearattention_pa_t_kernel(tc, hidden_states, Wq, Wk, gamma, be
 
         def normalise(block, first_tile):
             g, s = divmod(block, 2)
-            f_sb = f_pool.tile([P, RUN, HEADS * D], F32, name="f_sb")
-            for j in range(RUN):
+            for t in range(first_tile, first_tile + RUN):
+                f_sb = f_pool.tile([P, HEADS * D], F32, name="f_sb")
                 for h in range(HEADS):
-                    n = (first_tile + j) * HEADS + h
+                    n = t * HEADS + h
                     nc.vector.tensor_scalar(
-                        out=f_sb[:, j, h * D : (h + 1) * D],
-                        in0=u_sb[block][:, first_tile + j, h * D : (h + 1) * D],
+                        out=f_sb[:, h * D : (h + 1) * D],
+                        in0=u_sb[block][:, t, h * D : (h + 1) * D],
                         scalar1=mean[block][:, n : n + 1],
                         scalar2=rstd[block][:, n : n + 1],
                         op0=ALU.subtract,
                         op1=ALU.mult,
                     )
-            nc.sync.dma_start(out=out_dram[s][g][:, first_tile : first_tile + RUN, :], in_=f_sb[:])
+                nc.sync.dma_start(out=out_dram[s][g][:, t, :], in_=f_sb[:])
 
         for n in range(JOBS_FIRST):
             job_transpose(n)

@@ -94,7 +94,7 @@ def tile_rebasedlinearattention_pa_t_kernel(tc, hidden_states, Wq, Wk, gamma, be
         nc.vector.memset(eps_col[:, 0:1], D * LN_EPS)
         nc.vector.memset(eps_col[:, 1:2], LN_EPS)
         warm = const.tile([P, 1], F32)
-        nc.scalar.activation(out=warm[:], in_=eps_col[:, 0:1], func=ACT.Sqrt)
+        nc.scalar.activation(out=warm[:], in_=eps_col[:, 0:1], func=ACT.Abs_reciprocal_sqrt)
 
         job_bank = {}
         job_grouped = {}
@@ -120,10 +120,10 @@ def tile_rebasedlinearattention_pa_t_kernel(tc, hidden_states, Wq, Wk, gamma, be
 
         u_t = {}
         u_sb = {}
+        u_rows = {}
         stats = {}
         mean = {}
         m2 = {}
-        std = {}
         rstd = {}
 
         def project(block, first_head):
@@ -147,23 +147,29 @@ def tile_rebasedlinearattention_pa_t_kernel(tc, hidden_states, Wq, Wk, gamma, be
                     out=u_t[block][:, h, :], in_=acc[:], func=ACT.Identity, scale=gb_col[:, 0:1], bias=gb_col[:, 1:2]
                 )
 
-        def tokens_to_partitions(block, first_tile):
+        def tokens_to_partitions(block, first_tile, jobs_are_done):
             if first_tile == 0:
                 u_sb[block] = u_pool.tile([P, TILES, HEADS * D], F32, name="u_sb")
             for t in range(first_tile, first_tile + RUN):
-                bank = bt_psum.tile([P, HEADS * D], F32, name="bank")
+                stays = jobs_are_done and t == TILES - 1
+                if stays:
+                    bank = kt_psum.tile([P, HEADS * D], F32, name="kt")
+                else:
+                    bank = bt_psum.tile([P, HEADS * D], F32, name="bank")
                 for h in range(HEADS):
                     nc.tensor.transpose(bank[:, h * D : (h + 1) * D], u_t[block][:, h, t * P : (t + 1) * P], ident[:])
-                nc.scalar.copy(out=u_sb[block][:, t, :], in_=bank[:])
+                if stays:
+                    u_rows[block, t] = bank
+                else:
+                    nc.scalar.copy(out=u_sb[block][:, t, :], in_=bank[:])
+                    u_rows[block, t] = u_sb[block][:, t, :]
 
         def statistics(block, first_tile):
             if first_tile == 0:
                 stats[block] = small.tile([P, ROWS, 6], F32, name="stats")
             for t in range(first_tile, first_tile + RUN):
                 for h in range(HEADS):
-                    nc.vector.bn_stats(
-                        out=stats[block][:, t * HEADS + h, :], in_=u_sb[block][:, t, h * D : (h + 1) * D]
-                    )
+                    nc.vector.bn_stats(out=stats[block][:, t * HEADS + h, :], in_=u_rows[block, t][:, h * D : (h + 1) * D])
 
         def merge_halves(block):
             halves = stats[block][:].rearrange("p n (e k) -> p n e k", e=2)
@@ -186,20 +192,16 @@ def tile_rebasedlinearattention_pa_t_kernel(tc, hidden_states, Wq, Wk, gamma, be
                 out=mean[block][:], in0=mean_sum[:], scalar1=0.5, scalar2=0.0, op0=ALU.mult, op1=ALU.add
             )
 
-        def deviation(block):
+        def inverse_deviation(block):
             s = block % 2
-            std[block] = small.tile([P, ROWS], F32, name="std")
+            rstd[block] = small.tile([P, ROWS], F32, name="rstd")
             nc.scalar.activation(
-                out=std[block][:],
+                out=rstd[block][:],
                 in_=m2[block][:],
-                func=ACT.Sqrt,
+                func=ACT.Abs_reciprocal_sqrt,
                 scale=(1.0 if s == 0 else 1.0 / D),
                 bias=eps_col[:, s : s + 1],
             )
-
-        def invert(block):
-            rstd[block] = small.tile([P, ROWS], F32, name="rstd")
-            nc.vector.reciprocal(out=rstd[block][:], in_=std[block][:])
 
         def normalise(block, first_tile):
             g, s = divmod(block, 2)
@@ -209,7 +211,7 @@ def tile_rebasedlinearattention_pa_t_kernel(tc, hidden_states, Wq, Wk, gamma, be
                     n = t * HEADS + h
                     nc.vector.tensor_scalar(
                         out=f_sb[:, h * D : (h + 1) * D],
-                        in0=u_sb[block][:, t, h * D : (h + 1) * D],
+                        in0=u_rows[block, t][:, h * D : (h + 1) * D],
                         scalar1=mean[block][:, n : n + 1],
                         scalar2=rstd[block][:, n : n + 1],
                         op0=ALU.subtract,
@@ -244,11 +246,11 @@ def tile_rebasedlinearattention_pa_t_kernel(tc, hidden_states, Wq, Wk, gamma, be
         for j in range(N_ROUNDS + 7):
             fresh = range(done, min(done + JOBS_PER_ROUND, len(jobs)))
             if whole_block(j - 6) is not None:
-                deviation(whole_block(j - 6))
+                inverse_deviation(whole_block(j - 6))
             if part_of_block(j) is not None:
                 project(*part_of_block(j))
             if part_of_block(j - 2) is not None:
-                tokens_to_partitions(*part_of_block(j - 2))
+                tokens_to_partitions(*part_of_block(j - 2), len(fresh) == 0)
             for n in fresh:
                 job_transpose(n)
             for n in fresh:
@@ -267,5 +269,3 @@ def tile_rebasedlinearattention_pa_t_kernel(tc, hidden_states, Wq, Wk, gamma, be
                     job_group(n)
             if part_of_block(j - 7) is not None:
                 normalise(*part_of_block(j - 7))
-            if whole_block(j - 6) is not None:
-                invert(whole_block(j - 6))

from contextlib import ExitStack

import concourse.mybir as mybir
from concourse.masks import make_identity

F32 = mybir.dt.float32
BF16 = mybir.dt.bfloat16
U32 = mybir.dt.uint32
U8 = mybir.dt.uint8
FP8X4 = mybir.dt.float8_e4m3fn_x4
ALU = mybir.AluOpType
ACT = mybir.ActivationFunctionType

P = 128
TOKENS = 4 * 1024
HID = 1024
HEADS = 4
D = 128
LN_EPS = 1e-5
K_PASS = 4 * P
PASSES = HID // K_PASS
WORDS = K_PASS // 2
GROUP = 512
N_GROUPS = TOKENS // GROUP
TILES = GROUP // P
N_BLOCKS = 2 * N_GROUPS
ROWS = TILES * HEADS
RUN = 2
ROUNDS = HEADS // RUN
N_ROUNDS = N_BLOCKS * ROUNDS
JOBS_FIRST = 8
JOBS_PER_ROUND = 3

FLOPS = 2 * TOKENS * HID * 2 * HEADS * D


def tile_rebasedlinearattention_pa_t_kernel(tc, hidden_states, Wq, Wk, gamma, beta, out_0, out_1):
    nc = tc.nc
    x_dram = hidden_states.rearrange("b t k -> (b t) k").rearrange("(g p t) k -> g p t k", p=P, t=TILES)
    w_dram = [w.rearrange("(h p) k -> p h k", p=P) for w in (Wq, Wk)]
    out_dram = [
        o.rearrange("b t h d -> (b t) (h d)").rearrange("(g p t) f -> g p t f", p=P, t=TILES) for o in (out_0, out_1)
    ]

    with ExitStack() as stack:
        const = stack.enter_context(tc.tile_pool(name="const", bufs=1))
        raw_pool = stack.enter_context(tc.tile_pool(name="raw", bufs=10))
        grouped_pool = stack.enter_context(tc.tile_pool(name="grouped", bufs=6))
        ut_pool = stack.enter_context(tc.tile_pool(name="ut", bufs=2))
        u_pool = stack.enter_context(tc.tile_pool(name="u", bufs=4))
        f_pool = stack.enter_context(tc.tile_pool(name="f", bufs=8))
        small = stack.enter_context(tc.tile_pool(name="small", bufs=3))
        kt_psum = stack.enter_context(tc.psum_pool(name="kt", bufs=3))
        mx_psum = stack.enter_context(tc.psum_pool(name="mx", bufs=2))
        bt_psum = stack.enter_context(tc.psum_pool(name="bt", bufs=3))
        stack.enter_context(tc.manual_schedule())

        w_codes = const.tile([P, PASSES, 2 * HEADS * D], U32, align_bytes=64)
        w_scales = const.tile([P, PASSES, 2 * HEADS * D], U8, align_bytes=64)
        x_codes = const.tile([P, N_GROUPS, PASSES, GROUP], U32, align_bytes=64)
        x_scales = const.tile([P, N_GROUPS, PASSES, GROUP], U8, align_bytes=64)

        jobs = []

        def load_rows(rows_dram, codes, scales):
            raw = raw_pool.tile([P, 2, HID], BF16, name="raw")
            nc.sync.dma_start(out=raw[:], in_=rows_dram)
            for c in range(PASSES):
                jobs.append((raw[:].bitcast(F32), c, codes[:, c, :], scales[:, c, :]))

        def load_tokens(g):
            for t in range(0, TILES, 2):
                cols = slice(t * P, (t + 2) * P)
                load_rows(x_dram[g][:, t : t + 2, :], x_codes[:, g, :, cols], x_scales[:, g, :, cols])

        def load_weights(s):
            for h in range(0, HEADS, 2):
                cols = slice((s * HEADS + h) * D, (s * HEADS + h + 2) * D)
                load_rows(w_dram[s][:, h : h + 2, :], w_codes[:, :, cols], w_scales[:, :, cols])

        load_tokens(0)
        load_weights(0)
        gb_rows = const.tile([P, P], BF16)
        nc.vector.memset(gb_rows[:], 0.0)
        nc.sync.dma_start(out=gb_rows[0:1, :], in_=gamma.rearrange("(o d) -> o d", o=1))
        nc.sync.dma_start(out=gb_rows[1:2, :], in_=beta.rearrange("(o d) -> o d", o=1))
        load_weights(1)
        for g in range(1, N_GROUPS):
            load_tokens(g)

        ident = const.tile([P, P], F32)
        make_identity(nc, ident[:])
        eps_col = const.tile([P, 2], F32)
        nc.vector.memset(eps_col[:, 0:1], D * LN_EPS)
        nc.vector.memset(eps_col[:, 1:2], LN_EPS)
        warm = const.tile([P, 1], F32)
        nc.scalar.activation(out=warm[:], in_=eps_col[:, 0:1], func=ACT.Abs_reciprocal_sqrt)

        job_bank = {}
        job_grouped = {}

        def job_transpose(n):
            words, c, codes, scales = jobs[n]
            job_bank[n] = kt_psum.tile([P, 2, 2 * P], F32, name="kt")
            for u in range(2):
                for r in range(2):
                    first = c * WORDS + u * P
                    nc.tensor.transpose(job_bank[n][:, u, r * P : (r + 1) * P], words[:, r, first : first + P], ident[:])

        def job_group(n):
            job_grouped[n] = grouped_pool.tile([P, 2 * P, 4], BF16, align_bytes=64, name="grouped")
            engine_copy = nc.vector.tensor_copy if n % 2 == 0 else nc.scalar.copy
            engine_copy(out=job_grouped[n][:].bitcast(F32), in_=job_bank[n][:].rearrange("p u r -> p r u"))

        def job_quantise(n):
            words, c, codes, scales = jobs[n]
            nc.vector.quantize_mx(
                out=codes.bitcast(FP8X4), scales=scales, in_=job_grouped[n][:].rearrange("p r t -> p (r t)")
            )

        u_t = {}
        u_sb = {}
        u_rows = {}
        stats = {}
        mean = {}
        m2 = {}
        rstd = {}

        def project(block, first_head):
            g, s = divmod(block, 2)
            if first_head == 0:
                u_t[block] = ut_pool.tile([P, HEADS, GROUP], F32, name="u_t")
            for h in range(first_head, first_head + RUN):
                cols = slice((s * HEADS + h) * D, (s * HEADS + h + 1) * D)
                acc = mx_psum.tile([P, GROUP], F32, name="acc")
                for c in range(PASSES):
                    nc.tensor.matmul_mx(
                        out=acc[:],
                        lhsT=w_codes[:, c, cols].bitcast(FP8X4),
                        lhsT_scale=w_scales[:, c, cols],
                        rhs=x_codes[:, g, c, :].bitcast(FP8X4),
                        rhs_scale=x_scales[:, g, c, :],
                        start=(c == 0),
                        stop=(c == PASSES - 1),
                    )
                nc.scalar.activation(
                    out=u_t[block][:, h, :], in_=acc[:], func=ACT.Identity, scale=gb_col[:, 0:1], bias=gb_col[:, 1:2]
                )

        def tokens_to_partitions(block, first_tile, jobs_are_done):
            if first_tile == 0:
                u_sb[block] = u_pool.tile([P, TILES, HEADS * D], F32, name="u_sb")
            for t in range(first_tile, first_tile + RUN):
                stays = jobs_are_done and t == TILES - 1
                if stays:
                    bank = kt_psum.tile([P, HEADS * D], F32, name="kt")
                else:
                    bank = bt_psum.tile([P, HEADS * D], F32, name="bank")
                for h in range(HEADS):
                    nc.tensor.transpose(bank[:, h * D : (h + 1) * D], u_t[block][:, h, t * P : (t + 1) * P], ident[:])
                if stays:
                    u_rows[block, t] = bank
                else:
                    nc.scalar.copy(out=u_sb[block][:, t, :], in_=bank[:])
                    u_rows[block, t] = u_sb[block][:, t, :]

        def statistics(block, first_tile):
            if first_tile == 0:
                stats[block] = small.tile([P, ROWS, 6], F32, name="stats")
            for t in range(first_tile, first_tile + RUN):
                for h in range(HEADS):
                    nc.vector.bn_stats(out=stats[block][:, t * HEADS + h, :], in_=u_rows[block, t][:, h * D : (h + 1) * D])

        def merge_halves(block):
            halves = stats[block][:].rearrange("p n (e k) -> p n e k", e=2)
            gap = small.tile([P, ROWS], F32, name="gap")
            nc.gpsimd.tensor_sub(out=gap[:], in0=halves[:, :, 0, 1], in1=halves[:, :, 1, 1])
            within = small.tile([P, ROWS], F32, name="within")
            nc.gpsimd.tensor_add(out=within[:], in0=halves[:, :, 0, 2], in1=halves[:, :, 1, 2])
            gap_scaled = small.tile([P, ROWS], F32, name="gap_scaled")
            nc.gpsimd.tensor_scalar(
                out=gap_scaled[:], in0=gap[:], scalar1=D / 4.0, scalar2=0.0, op0=ALU.mult, op1=ALU.add
            )
            between = small.tile([P, ROWS], F32, name="between")
            nc.gpsimd.tensor_mul(out=between[:], in0=gap_scaled[:], in1=gap[:])
            m2[block] = small.tile([P, ROWS], F32, name="m2")
            nc.gpsimd.tensor_add(out=m2[block][:], in0=between[:], in1=within[:])
            mean_sum = small.tile([P, ROWS], F32, name="mean_sum")
            nc.gpsimd.tensor_add(out=mean_sum[:], in0=halves[:, :, 0, 1], in1=halves[:, :, 1, 1])
            mean[block] = small.tile([P, ROWS], F32, name="mean")
            nc.gpsimd.tensor_scalar(
                out=mean[block][:], in0=mean_sum[:], scalar1=0.5, scalar2=0.0, op0=ALU.mult, op1=ALU.add
            )

        def inverse_deviation(block):
            s = block % 2
            rstd[block] = small.tile([P, ROWS], F32, name="rstd")
            nc.scalar.activation(
                out=rstd[block][:],
                in_=m2[block][:],
                func=ACT.Abs_reciprocal_sqrt,
                scale=(1.0 if s == 0 else 1.0 / D),
                bias=eps_col[:, s : s + 1],
            )

        def normalise(block, first_tile):
            g, s = divmod(block, 2)
            for t in range(first_tile, first_tile + RUN):
                f_sb = f_pool.tile([P, HEADS * D], F32, name="f_sb")
                for h in range(HEADS):
                    n = t * HEADS + h
                    nc.vector.tensor_scalar(
                        out=f_sb[:, h * D : (h + 1) * D],
                        in0=u_rows[block, t][:, h * D : (h + 1) * D],
                        scalar1=mean[block][:, n : n + 1],
                        scalar2=rstd[block][:, n : n + 1],
                        op0=ALU.subtract,
                        op1=ALU.mult,
                    )
                nc.sync.dma_start(out=out_dram[s][g][:, t, :], in_=f_sb[:])

        for n in range(JOBS_FIRST):
            job_transpose(n)
            job_group(n)
            if n > 0:
                job_quantise(n - 1)
        gb_f32 = const.tile([P, P], F32)
        nc.vector.tensor_copy(out=gb_f32[:], in_=gb_rows[:])
        gb_bank = kt_psum.tile([P, 2, 2 * P], F32, name="kt")
        nc.tensor.transpose(gb_bank[:, 0, 0:P], gb_f32[:], ident[:])
        gb_col = const.tile([P, 2], F32)
        nc.vector.tensor_copy(out=gb_col[:], in_=gb_bank[:, 0, 0:2])

        def part_of_block(r):
            if 0 <= r < N_ROUNDS:
                return r // ROUNDS, (r % ROUNDS) * RUN
            return None

        def whole_block(r):
            if 0 <= r < N_ROUNDS and r % ROUNDS == 0:
                return r // ROUNDS
            return None

        done = JOBS_FIRST
        quantised = JOBS_FIRST - 1
        for j in range(N_ROUNDS + 7):
            fresh = range(done, min(done + JOBS_PER_ROUND, len(jobs)))
            if whole_block(j - 6) is not None:
                inverse_deviation(whole_block(j - 6))
            if part_of_block(j) is not None:
                project(*part_of_block(j))
            if part_of_block(j - 2) is not None:
                tokens_to_partitions(*part_of_block(j - 2), len(fresh) == 0)
            for n in fresh:
                job_transpose(n)
            for n in fresh:
                if n % 2 == 1:
                    job_group(n)
            for n in range(quantised, done):
                job_quantise(n)
            quantised = done
            done = done + len(fresh)
            if part_of_block(j - 3) is not None:
                statistics(*part_of_block(j - 3))
            if whole_block(j - 4) is not None:
                merge_halves(whole_block(j - 4))
            for n in fresh:
                if n % 2 == 0:
                    job_group(n)
            if part_of_block(j - 7) is not None:
                normalise(*part_of_block(j - 7))
